import numpy as np
import ml_dtypes


def mxq(x, axis, fmt="e4m3"):
    dtype, down = {"e4m3": (ml_dtypes.float8_e4m3fn, 7), "e5m2": (ml_dtypes.float8_e5m2, 14)}[fmt]
    v = np.moveaxis(np.asarray(x, np.float32).astype(ml_dtypes.bfloat16).astype(np.float64), axis, -1)
    blocks = v.reshape(v.shape[:-1] + (-1, 32))
    amax = np.abs(blocks).max(-1, keepdims=True)
    byte = np.maximum(np.where(amax > 0, np.frexp(amax)[1] - 1 + 127, 0) - down, 1)
    scale = np.exp2(byte - 127.0)
    codes = (blocks / scale).astype(np.float32).astype(dtype).astype(np.float64)
    return np.moveaxis((codes * scale).reshape(v.shape), -1, axis)


WIDE = False


def mx_kscale(k):
    if not WIDE:
        return np.ones(k)
    levels = np.array([10, -10, 5, -5, 0])
    if k % 512:
        return np.exp2(np.random.permutation(np.resize(levels, k // 32))).repeat(32)
    a = np.empty((k // 512, 16))
    for p in range(k // 512):
        a[p, :8] = np.random.permutation(np.resize(levels, 8))
        for g in range(8):
            far = levels[np.abs(levels - a[p, g]) >= 10]
            a[p, g + 8] = far[np.random.randint(len(far))]
    return np.exp2(a.ravel()).repeat(32)


BF16 = ml_dtypes.bfloat16


def bf(x):
    return np.asarray(x, np.float32).astype(BF16)


def f64(x):
    return np.asarray(x).astype(np.float64)


B, S, D, K, O, DEG, BLK = 4, 1024, 1024, 1024, 2048, 4, 512
HALF = DEG // 2
STEP = K // DEG


def make_masks(lo, hi):
    rows = np.arange(K)
    deg_r = (rows * DEG) // K + 1
    degmask = (np.arange(1, DEG + 1)[:, None] <= deg_r[None, :]) * 1.0
    tri_l = np.tril(np.ones((K, D)))
    tri_u = np.triu(np.ones((K, D)))
    return np.stack([degmask[i][:, None] * (tri_l if i % 2 == 0 else tri_u) for i in range(lo, hi)])


def factor(zq, Wi, i):
    y = np.zeros((zq.shape[0], K))
    for j in range(K // BLK):
        a, b = max(j * BLK, i * STEP), (j + 1) * BLK
        c0, c1 = (0, min(b, D)) if i % 2 == 0 else (j * BLK, D)
        if a >= b or c0 >= c1:
            continue
        y[:, a:b] = zq[:, c0:c1] @ mxq(Wi[a:b, c0:c1], 1, "e4m3").T
    return y


def setup_inputs():
    s = mx_kscale(D)
    return {"z": bf(np.random.standard_normal((B, S, D)) * s),
            "U_lo": bf(np.random.standard_normal((HALF, K, D)) / np.sqrt(D) / s),
            "masks_lo": bf(make_masks(0, HALF))}


def reference(z, U_lo, masks_lo):
    zq = mxq(f64(z).reshape(-1, D), 1, "e4m3")
    W = f64(masks_lo) * f64(U_lo)
    out = factor(zq, W[0], 0)
    for i in range(1, HALF):
        out = factor(zq, W[i], i) * out + out
    return out

@@ -1,0 +1,395 @@
+from contextlib import ExitStack
+
+import concourse.mybir as mybir
+from concourse.masks import make_identity
+
+F32 = mybir.dt.float32
+BF16 = mybir.dt.bfloat16
+U32 = mybir.dt.uint32
+U8 = mybir.dt.uint8
+FP8X4 = mybir.dt.float8_e4m3fn_x4
+ALU = mybir.AluOpType
+
+P = 128
+TOKENS = 4096
+FEATS = 1024
+RANKS = 1024
+GROUP = 4
+N_GROUPS = TOKENS // (P * GROUP)
+
+FLOPS = 2 * TOKENS * 1310720
+BYTES = TOKENS * FEATS * 2 + TOKENS * RANKS * 4 + 2 * 1310720 * 2
+
+GENERAL = False
+PIN = True
+ZCOPY = "svsv"
+OUT_BUFS = 6
+RUN_GROUPS = 2
+FINE_PAIRS = 3
+
+W_BANKS = [
+    (0, 0, 0, 0, 0),
+    (0, 0, 1, 0, 1),
+    (1, 0, 1, 1, 0),
+    (1, 1, 1, 1, 1),
+    (0, 0, 2, 2, 0),
+    (0, 0, 3, 2, 1),
+    (0, 1, 2, 3, 0),
+    (0, 1, 3, 3, 1),
+    (1, 1, 2, 4, 0),
+    (1, 1, 3, 4, 1),
+]
+
+
+def spec_range(i, rp):
+    if i == 0:
+        return (0, 512) if rp < 2 else (0, 1024)
+    return (0, 1024) if rp == 1 else (512, 1024)
+
+
+def live_range(i, rp):
+    if GENERAL:
+        return spec_range(i, rp)
+    return (0, 256 * (rp + 1)) if i == 0 else (256 * rp, 1024)
+
+
+def mask_range(i, rp):
+    if GENERAL:
+        return spec_range(i, rp)
+    return (256 * rp, 256 * rp + 256)
+
+
+def tile_cp_sparse_degree_lu_pa_t_kernel(tc, z, U_lo, masks_lo, out):
+    nc = tc.nc
+    zf = z.flatten_outer_dims()
+    with ExitStack() as ctx:
+        const = ctx.enter_context(tc.tile_pool(name="const", bufs=1))
+        zin = ctx.enter_context(tc.tile_pool(name="zin", bufs=N_GROUPS))
+        zwork = ctx.enter_context(tc.tile_pool(name="zwork", bufs=3))
+        outp = ctx.enter_context(tc.tile_pool(name="outp", bufs=OUT_BUFS))
+        psum = ctx.enter_context(tc.psum_pool(name="psum", bufs=8))
+        if PIN:
+            ctx.enter_context(tc.manual_schedule())
+
+        count = [0]
+
+        def bank():
+            count[0] += 1
+            return psum.tile([P, 512], F32, name="bank%d" % count[0], tag="bank")
+
+        def copy_out(eng, dst, src):
+            if eng == "s":
+                nc.scalar.copy(out=dst, in_=src)
+            else:
+                nc.vector.tensor_copy(out=dst, in_=src)
+
+        ident = const.tile([P, P], F32, name="ident")
+        make_identity(nc, ident[:])
+
+        pairs_a = [(0, 0), (0, 1), (1, 1)]
+        pairs_b = [(0, 2), (0, 3), (1, 2), (1, 3)]
+        raws = {}
+        msks = {}
+        for key in pairs_a + pairs_b:
+            i, rp = key
+            s0, s1 = spec_range(i, rp)
+            m0, m1 = mask_range(i, rp)
+            raws[key] = const.tile([P, 2 * (s1 - s0)], BF16, name="raw%d%d" % key)
+            msks[key] = const.tile([P, 2 * (m1 - m0)], BF16, name="msk%d%d" % key)
+            l0, l1 = live_range(i, rp)
+            r3 = raws[key][:].rearrange("p (r c) -> p r c", r=2)
+            if l0 > s0:
+                nc.vector.memset(r3[:, :, 0 : l0 - s0], 0.0)
+            if l1 < s1:
+                nc.vector.memset(r3[:, :, l1 - s0 : s1 - s0], 0.0)
+        wg = [const.tile([P, 2048], BF16, name="wg%d" % s, align_bytes=64) for s in range(5)]
+        wc = [const.tile([P, 512], U32, name="wc%d" % s, align_bytes=64) for s in range(5)]
+        ws = [const.tile([P, 512], U8, name="ws%d" % s, align_bytes=64) for s in range(5)]
+
+        def load_w(key):
+            i, rp = key
+            s0, s1 = spec_range(i, rp)
+            m0, m1 = mask_range(i, rp)
+            l0, l1 = live_range(i, rp)
+            rows = slice(256 * rp, 256 * rp + 256)
+            nc.sync.dma_start(
+                out=msks[key][:].rearrange("p (r c) -> p r c", r=2),
+                in_=masks_lo[i, rows, m0:m1].rearrange("(r p) c -> p r c", p=P),
+            )
+            nc.sync.dma_start(
+                out=raws[key][:].rearrange("p (r c) -> p r c", r=2)[:, :, l0 - s0 : l1 - s0],
+                in_=U_lo[i, rows, l0:l1].rearrange("(r p) c -> p r c", p=P),
+            )
+
+        zraw = [zin.tile([P, GROUP * FEATS], BF16, name="zraw%d" % g, tag="zraw") for g in range(N_GROUPS)]
+
+        def load_z(grp, j0, j1):
+            src = zf[512 * grp : 512 * grp + 512, :].rearrange("(p j) c -> p j c", j=GROUP)
+            dst = zraw[grp][:].rearrange("p (j c) -> p j c", j=GROUP)
+            nc.sync.dma_start(out=dst[:, j0:j1, :], in_=src[:, j0:j1, :])
+
+        for key in pairs_a:
+            load_w(key)
+        load_z(0, 0, 2)
+        load_z(0, 2, 4)
+        for key in pairs_b:
+            load_w(key)
+        for grp in range(1, N_GROUPS):
+            load_z(grp, 0, GROUP)
+
+        def mask_mult(i, rp):
+            s0, s1 = spec_range(i, rp)
+            m0, m1 = mask_range(i, rp)
+            part = raws[(i, rp)][:].rearrange("p (r c) -> p r c", r=2)[:, :, m0 - s0 : m1 - s0]
+            nc.vector.tensor_tensor(
+                out=part, in0=part, in1=msks[(i, rp)][:].rearrange("p (r c) -> p r c", r=2), op=ALU.mult
+            )
+
+        held = {}
+
+        def w_transposes(n):
+            i, g, rp, s, half = W_BANKS[n]
+            s0, s1 = spec_range(i, rp)
+            words = (s1 - s0) // 2
+            rawf = raws[(i, rp)][:].bitcast(F32)
+            bk = bank()
+            for u in range(2):
+                for r in range(2):
+                    w0 = r * words + (512 * g - s0) // 2 + u
+                    nc.tensor.transpose(
+                        out=bk[:, 256 * u + P * r : 256 * u + P * r + P],
+                        in_=rawf[:, w0 : w0 + 2 * P - 1 : 2],
+                        identity=ident[:],
+                    )
+            held[("w", n)] = bk
+
+        def w_copy(n, eng):
+            i, g, rp, s, half = W_BANKS[n]
+            copy_out(
+                eng,
+                wg[s][:].bitcast(F32)[:, 512 * half : 512 * half + 512].rearrange("p (r u) -> p r u", u=2),
+                held[("w", n)][:].rearrange("p (u r) -> p r u", u=2),
+            )
+
+        def w_quant(s):
+            nc.vector.quantize_mx(out=wc[s][:].bitcast(FP8X4), scales=ws[s][:], in_=wg[s][:])
+
+        zg = {}
+        zc = {}
+        zs = {}
+
+        def z_transposes(grp, j):
+            if j == 0:
+                zg[grp] = zwork.tile([P, GROUP * FEATS], BF16, name="zg%d" % grp, tag="zg", align_bytes=64)
+                zc[grp] = zwork.tile([P, GROUP * 256], U32, name="zc%d" % grp, tag="zc", align_bytes=64)
+                zs[grp] = zwork.tile([P, GROUP * 256], U8, name="zs%d" % grp, tag="zs", align_bytes=64)
+            zrf = zraw[grp][:].bitcast(F32)
+            bk = bank()
+            for c in range(4):
+                w0 = 512 * j + 256 * (c // 2) + c % 2
+                nc.tensor.transpose(
+                    out=bk[:, P * c : P * c + P], in_=zrf[:, w0 : w0 + 2 * P - 1 : 2], identity=ident[:]
+                )
+            held[("z", grp, j)] = bk
+
+        def z_copy(grp, j, eng):
+            copy_out(
+                eng,
+                zg[grp][:].bitcast(F32)[:, 512 * j : 512 * j + 512].rearrange("p (g t u) -> p g t u", g=2, u=2),
+                held[("z", grp, j)][:].rearrange("p (g u t) -> p g t u", g=2, u=2),
+            )
+
+        def z_quant(grp, h):
+            nc.vector.quantize_mx(
+                out=zc[grp][:, 512 * h : 512 * h + 512].bitcast(FP8X4),
+                scales=zs[grp][:, 512 * h : 512 * h + 512],
+                in_=zg[grp][:, 2048 * h : 2048 * h + 2048],
+            )
+
+        def mm(dst, grp, j, g, s, c0, c1, start, stop):
+            a = 256 * j + P * g
+            nc.tensor.matmul_mx(
+                out=dst,
+                lhsT=zc[grp][:, a : a + P].bitcast(FP8X4),
+                lhsT_scale=zs[grp][:, a : a + P],
+                rhs=wc[s][:, c0:c1].bitcast(FP8X4),
+                rhs_scale=ws[s][:, c0:c1],
+                start=start,
+                stop=stop,
+            )
+
+        osb = {}
+
+        def mx_y0a(grp, h):
+            for jj in range(2):
+                bk = bank()
+                mm(bk[:], grp, 2 * h + jj, 0, 0, 0, 512, True, True)
+                held[("y0a", grp, h, jj)] = bk
+
+        def mx_y1a(grp, h):
+            bk = bank()
+            for jj in range(2):
+                mm(bk[:, 256 * jj : 256 * jj + 256], grp, 2 * h + jj, 0, 1, 0, 256, True, False)
+                mm(bk[:, 256 * jj : 256 * jj + 256], grp, 2 * h + jj, 1, 1, 256, 512, False, True)
+            held[("y1a", grp, h)] = bk
+
+        def mx_y0b(grp, h, jj):
+            bk = bank()
+            mm(bk[:], grp, 2 * h + jj, 0, 2, 0, 512, True, False)
+            mm(bk[:], grp, 2 * h + jj, 1, 3, 0, 512, False, True)
+            held[("y0b", grp, h, jj)] = bk
+
+        def mx_y1b(grp, h, jj):
+            bk = bank()
+            mm(bk[:], grp, 2 * h + jj, 1, 4, 0, 512, True, True)
+            held[("y1b", grp, h, jj)] = bk
+
+        def out_y0a(grp, h):
+            o = outp.tile([P, 2 * RANKS], F32, name="o%d%d" % (grp, h), tag="o")
+            osb[(grp, h)] = o
+            for jj in range(2):
+                nc.scalar.copy(out=o[:, RANKS * jj : RANKS * jj + 512], in_=held[("y0a", grp, h, jj)][:])
+
+        def out_y1a(grp, h):
+            o3 = osb[(grp, h)][:].rearrange("p (j r) -> p j r", j=2)[:, :, 256:512]
+            nc.vector.scalar_tensor_tensor(
+                out=o3,
+                in0=held[("y1a", grp, h)][:].rearrange("p (j r) -> p j r", j=2),
+                scalar=1.0,
+                in1=o3,
+                op0=ALU.add,
+                op1=ALU.mult,
+            )
+
+        def out_y0b(grp, h, jj):
+            nc.scalar.copy(
+                out=osb[(grp, h)][:, RANKS * jj + 512 : RANKS * jj + 1024], in_=held[("y0b", grp, h, jj)][:]
+            )
+
+        def out_y1b(grp, h, jj):
+            part = osb[(grp, h)][:, RANKS * jj + 512 : RANKS * jj + 1024]
+            nc.vector.scalar_tensor_tensor(
+                out=part, in0=held[("y1b", grp, h, jj)][:], scalar=1.0, in1=part, op0=ALU.add, op1=ALU.mult
+            )
+
+        def store(grp, h, j0, j1, r0, r1):
+            dst = out[512 * grp : 512 * grp + 512, :].rearrange("(p j) r -> p j r", j=GROUP)
+            src = osb[(grp, h)][:].rearrange("p (j r) -> p j r", j=2)
+            nc.sync.dma_start(out=dst[:, 2 * h + j0 : 2 * h + j1, r0:r1], in_=src[:, j0:j1, r0:r1])
+
+        def store_pair(grp, h):
+            store(grp, h, 0, 2, 0, RANKS)
+
+        def pair(grp, h):
+            fine = 2 * (N_GROUPS - 1 - grp) + (1 - h) < FINE_PAIRS
+            mx_y0a(grp, h)
+            mx_y1a(grp, h)
+            out_y0a(grp, h)
+            out_y1a(grp, h)
+            if fine:
+                store(grp, h, 0, 2, 0, 512)
+            for jj in range(2):
+                mx_y0b(grp, h, jj)
+            for jj in range(2):
+                mx_y1b(grp, h, jj)
+            for jj in range(2):
+                out_y0b(grp, h, jj)
+            for jj in range(2):
+                out_y1b(grp, h, jj)
+                if fine:
+                    store(grp, h, jj, jj + 1, 512, RANKS)
+            if not fine:
+                store_pair(grp, h)
+
+        mask_mult(0, 0)
+        w_transposes(0)
+        mask_mult(0, 1)
+        w_copy(0, "v")
+        mask_mult(1, 1)
+        w_transposes(1)
+        w_transposes(2)
+        w_transposes(3)
+        w_copy(1, "s")
+        w_copy(2, "s")
+        w_quant(0)
+        z_transposes(0, 0)
+        z_transposes(0, 1)
+        z_copy(0, 1, "v")
+        z_copy(0, 0, "s")
+        w_copy(3, "s")
+        z_transposes(0, 2)
+        z_transposes(0, 3)
+        z_quant(0, 0)
+        w_quant(1)
+        z_copy(0, 2, "s")
+        z_copy(0, 3, "s")
+        mask_mult(0, 2)
+        mx_y0a(0, 0)
+        mx_y1a(0, 0)
+        z_quant(0, 1)
+        out_y0a(0, 0)
+        mask_mult(0, 3)
+        out_y1a(0, 0)
+        mx_y0a(0, 1)
+        mx_y1a(0, 1)
+        out_y0a(0, 1)
+        mask_mult(1, 2)
+        mask_mult(1, 3)
+        w_transposes(4)
+        w_transposes(5)
+        w_transposes(6)
+        w_transposes(7)
+        w_transposes(8)
+        w_transposes(9)
+        out_y1a(0, 1)
+        w_copy(4, "s")
+        w_copy(5, "v")
+        w_copy(6, "s")
+        w_copy(7, "v")
+        w_quant(2)
+        w_copy(8, "s")
+        w_copy(9, "s")
+        w_quant(3)
+        z_transposes(1, 0)
+        z_transposes(1, 1)
+        z_transposes(1, 2)
+        z_transposes(1, 3)
+        w_quant(4)
+        z_copy(1, 0, "s")
+        z_copy(1, 1, "v")
+        z_copy(1, 2, "s")
+        z_copy(1, 3, "v")
+        mx_y0b(0, 0, 0)
+        mx_y0b(0, 0, 1)
+        mx_y1b(0, 0, 0)
+        mx_y1b(0, 0, 1)
+        out_y0b(0, 0, 0)
+        out_y0b(0, 0, 1)
+        z_quant(1, 0)
+        out_y1b(0, 0, 0)
+        out_y1b(0, 0, 1)
+        store_pair(0, 0)
+        mx_y0b(0, 1, 0)
+        mx_y0b(0, 1, 1)
+        mx_y1b(0, 1, 0)
+        mx_y1b(0, 1, 1)
+        out_y0b(0, 1, 0)
+        out_y0b(0, 1, 1)
+        z_quant(1, 1)
+        out_y1b(0, 1, 0)
+        out_y1b(0, 1, 1)
+        store_pair(0, 1)
+        for first in range(1, N_GROUPS, RUN_GROUPS):
+            ahead = [g for g in range(first + 1, first + 1 + RUN_GROUPS) if g < N_GROUPS]
+            for g in ahead:
+                for j in range(GROUP):
+                    z_transposes(g, j)
+            for g in ahead:
+                for j in range(GROUP):
+                    z_copy(g, j, ZCOPY[j])
+            todo = [(g, h) for g in ahead for h in range(2)]
+            now = [(g, h) for g in range(first, first + RUN_GROUPS) if g < N_GROUPS for h in range(2)]
+            for k in range(len(now)):
+                pair(now[k][0], now[k][1])
+                if k < len(todo):
+                    z_quant(todo[k][0], todo[k][1])

@@ -66,6 +66,7 @@ def tile_cp_sparse_degree_lu_pa_t_kernel(tc, z, U_lo, masks_lo, out):
         const = ctx.enter_context(tc.tile_pool(name="const", bufs=1))
         zin = ctx.enter_context(tc.tile_pool(name="zin", bufs=N_GROUPS))
         zwork = ctx.enter_context(tc.tile_pool(name="zwork", bufs=3))
+        zrun = ctx.enter_context(tc.tile_pool(name="zrun", bufs=4))
         outp = ctx.enter_context(tc.tile_pool(name="outp", bufs=OUT_BUFS))
         psum = ctx.enter_context(tc.psum_pool(name="psum", bufs=8))
         if PIN:
@@ -174,9 +175,20 @@ def tile_cp_sparse_degree_lu_pa_t_kernel(tc, z, U_lo, masks_lo, out):
         def w_quant(s):
             nc.vector.quantize_mx(out=wc[s][:].bitcast(FP8X4), scales=ws[s][:], in_=wg[s][:])
 
+        zr = {}
         zg = {}
         zc = {}
         zs = {}
+
+        def z_reorder(grp, h):
+            t = zrun.tile([P, 2 * FEATS], BF16, name="zr%d%d" % (grp, h), tag="zr")
+            nc.vector.tensor_copy(
+                out=t[:].bitcast(F32).rearrange("p (g u q) -> p g u q", g=4, u=2),
+                in_=zraw[grp][:, 2 * FEATS * h : 2 * FEATS * (h + 1)]
+                .bitcast(F32)
+                .rearrange("p (g q u) -> p g u q", g=4, u=2),
+            )
+            zr[(grp, h)] = t
 
         def z_transposes(grp, j):
             if j == 0:
@@ -186,10 +198,13 @@ def tile_cp_sparse_degree_lu_pa_t_kernel(tc, z, U_lo, masks_lo, out):
             zrf = zraw[grp][:].bitcast(F32)
             bk = bank()
             for c in range(4):
-                w0 = 512 * j + 256 * (c // 2) + c % 2
-                nc.tensor.transpose(
-                    out=bk[:, P * c : P * c + P], in_=zrf[:, w0 : w0 + 2 * P - 1 : 2], identity=ident[:]
-                )
+                if (grp, j // 2) in zr:
+                    w0 = 512 * (j % 2) + P * c
+                    words = zr[(grp, j // 2)][:].bitcast(F32)[:, w0 : w0 + P]
+                else:
+                    w0 = 512 * j + 256 * (c // 2) + c % 2
+                    words = zrf[:, w0 : w0 + 2 * P - 1 : 2]
+                nc.tensor.transpose(out=bk[:, P * c : P * c + P], in_=words, identity=ident[:])
             held[("z", grp, j)] = bk
 
         def z_copy(grp, j, eng):
@@ -376,6 +391,9 @@ def tile_cp_sparse_degree_lu_pa_t_kernel(tc, z, U_lo, masks_lo, out):
         out_y0b(0, 1, 0)
         out_y0b(0, 1, 1)
         z_quant(1, 1)
+        for g in range(2, 2 + RUN_GROUPS):
+            for h in range(2):
+                z_reorder(g, h)
         out_y1b(0, 1, 0)
         out_y1b(0, 1, 1)
         store_pair(0, 1)
@@ -389,7 +407,10 @@ def tile_cp_sparse_degree_lu_pa_t_kernel(tc, z, U_lo, masks_lo, out):
                     z_copy(g, j, ZCOPY[j])
             todo = [(g, h) for g in ahead for h in range(2)]
             now = [(g, h) for g in range(first, first + RUN_GROUPS) if g < N_GROUPS for h in range(2)]
+            later = [(g + RUN_GROUPS, h) for g, h in todo if g + RUN_GROUPS < N_GROUPS]
             for k in range(len(now)):
                 pair(now[k][0], now[k][1])
+                if k < len(later):
+                    z_reorder(later[k][0], later[k][1])
                 if k < len(todo):
                     z_quant(todo[k][0], todo[k][1])

@@ -22,9 +22,7 @@ BYTES = TOKENS * FEATS * 2 + TOKENS * RANKS * 4 + 2 * 1310720 * 2
 
 GENERAL = False
 PIN = True
-ZCOPY = "svsv"
 OUT_BUFS = 6
-RUN_GROUPS = 2
 FINE_PAIRS = 3
 
 W_BANKS = [
@@ -295,25 +293,33 @@ def tile_cp_sparse_degree_lu_pa_t_kernel(tc, z, U_lo, masks_lo, out):
         def store_pair(grp, h):
             store(grp, h, 0, 2, 0, RANKS)
 
-        def pair(grp, h):
-            fine = 2 * (N_GROUPS - 1 - grp) + (1 - h) < FINE_PAIRS
+        def is_fine(grp, h):
+            return 2 * (N_GROUPS - 1 - grp) + (1 - h) < FINE_PAIRS
+
+        def mx_a(grp, h):
             mx_y0a(grp, h)
             mx_y1a(grp, h)
+
+        def out_a(grp, h):
             out_y0a(grp, h)
             out_y1a(grp, h)
-            if fine:
+            if is_fine(grp, h):
                 store(grp, h, 0, 2, 0, 512)
+
+        def mx_b(grp, h):
             for jj in range(2):
                 mx_y0b(grp, h, jj)
             for jj in range(2):
                 mx_y1b(grp, h, jj)
+
+        def out_b(grp, h):
             for jj in range(2):
                 out_y0b(grp, h, jj)
             for jj in range(2):
                 out_y1b(grp, h, jj)
-                if fine:
+                if is_fine(grp, h):
                     store(grp, h, jj, jj + 1, 512, RANKS)
-            if not fine:
+            if not is_fine(grp, h):
                 store_pair(grp, h)
 
         mask_mult(0, 0)
@@ -339,78 +345,54 @@ def tile_cp_sparse_degree_lu_pa_t_kernel(tc, z, U_lo, masks_lo, out):
         z_copy(0, 2, "s")
         z_copy(0, 3, "s")
         mask_mult(0, 2)
-        mx_y0a(0, 0)
-        mx_y1a(0, 0)
-        z_quant(0, 1)
-        out_y0a(0, 0)
         mask_mult(0, 3)
+        mx_a(0, 0)
+        out_y0a(0, 0)
+        z_quant(0, 1)
+        for n in range(4, 8):
+            w_transposes(n)
         out_y1a(0, 0)
-        mx_y0a(0, 1)
-        mx_y1a(0, 1)
-        out_y0a(0, 1)
         mask_mult(1, 2)
         mask_mult(1, 3)
-        w_transposes(4)
-        w_transposes(5)
-        w_transposes(6)
-        w_transposes(7)
-        w_transposes(8)
-        w_transposes(9)
-        out_y1a(0, 1)
         w_copy(4, "s")
         w_copy(5, "v")
+        mx_a(0, 1)
         w_copy(6, "s")
         w_copy(7, "v")
+        w_transposes(8)
+        w_transposes(9)
         w_quant(2)
+        out_y0a(0, 1)
+        out_y1a(0, 1)
         w_copy(8, "s")
         w_copy(9, "s")
         w_quant(3)
-        z_transposes(1, 0)
-        z_transposes(1, 1)
-        z_transposes(1, 2)
-        z_transposes(1, 3)
+        for j in range(GROUP):
+            z_transposes(1, j)
         w_quant(4)
-        z_copy(1, 0, "s")
-        z_copy(1, 1, "v")
-        z_copy(1, 2, "s")
-        z_copy(1, 3, "v")
-        mx_y0b(0, 0, 0)
-        mx_y0b(0, 0, 1)
-        mx_y1b(0, 0, 0)
-        mx_y1b(0, 0, 1)
-        out_y0b(0, 0, 0)
-        out_y0b(0, 0, 1)
+        for j in range(GROUP):
+            z_copy(1, j, "svsv"[j])
+        mx_b(0, 0)
         z_quant(1, 0)
-        out_y1b(0, 0, 0)
-        out_y1b(0, 0, 1)
-        store_pair(0, 0)
-        mx_y0b(0, 1, 0)
-        mx_y0b(0, 1, 1)
-        mx_y1b(0, 1, 0)
-        mx_y1b(0, 1, 1)
-        out_y0b(0, 1, 0)
-        out_y0b(0, 1, 1)
+        out_b(0, 0)
+        z_reorder(2, 0)
+        z_reorder(2, 1)
+        mx_b(0, 1)
         z_quant(1, 1)
-        for g in range(2, 2 + RUN_GROUPS):
+        out_b(0, 1)
+        for first in range(1, N_GROUPS):
+            nxt = first + 1
+            if nxt < N_GROUPS:
+                for j in range(GROUP):
+                    z_transposes(nxt, j)
+                for j in range(GROUP):
+                    z_copy(nxt, j, "svsv"[j])
             for h in range(2):
-                z_reorder(g, h)
-        out_y1b(0, 1, 0)
-        out_y1b(0, 1, 1)
-        store_pair(0, 1)
-        for first in range(1, N_GROUPS, RUN_GROUPS):
-            ahead = [g for g in range(first + 1, first + 1 + RUN_GROUPS) if g < N_GROUPS]
-            for g in ahead:
-                for j in range(GROUP):
-                    z_transposes(g, j)
-            for g in ahead:
-                for j in range(GROUP):
-                    z_copy(g, j, ZCOPY[j])
-            todo = [(g, h) for g in ahead for h in range(2)]
-            now = [(g, h) for g in range(first, first + RUN_GROUPS) if g < N_GROUPS for h in range(2)]
-            later = [(g + RUN_GROUPS, h) for g, h in todo if g + RUN_GROUPS < N_GROUPS]
-            for k in range(len(now)):
-                pair(now[k][0], now[k][1])
-                if k < len(later):
-                    z_reorder(later[k][0], later[k][1])
-                if k < len(todo):
-                    z_quant(todo[k][0], todo[k][1])
+                mx_a(first, h)
+                out_a(first, h)
+                if nxt + 1 < N_GROUPS:
+                    z_reorder(nxt + 1, h)
+                mx_b(first, h)
+                if nxt < N_GROUPS:
+                    z_quant(nxt, h)
+                out_b(first, h)

@@ -20,41 +20,30 @@ N_GROUPS = TOKENS // (P * GROUP)
 FLOPS = 2 * TOKENS * 1310720
 BYTES = TOKENS * FEATS * 2 + TOKENS * RANKS * 4 + 2 * 1310720 * 2
 
-GENERAL = False
-PIN = True
 OUT_BUFS = 6
 FINE_PAIRS = 3
 
-W_BANKS = [
-    (0, 0, 0, 0, 0),
-    (0, 0, 1, 0, 1),
-    (1, 0, 1, 1, 0),
-    (1, 1, 1, 1, 1),
-    (0, 0, 2, 2, 0),
-    (0, 0, 3, 2, 1),
-    (0, 1, 2, 3, 0),
-    (0, 1, 3, 3, 1),
-    (1, 1, 2, 4, 0),
-    (1, 1, 3, 4, 1),
-]
-
-
-def spec_range(i, rp):
-    if i == 0:
-        return (0, 512) if rp < 2 else (0, 1024)
-    return (0, 1024) if rp == 1 else (512, 1024)
-
-
-def live_range(i, rp):
-    if GENERAL:
-        return spec_range(i, rp)
-    return (0, 256 * (rp + 1)) if i == 0 else (256 * rp, 1024)
-
-
-def mask_range(i, rp):
-    if GENERAL:
-        return spec_range(i, rp)
-    return (256 * rp, 256 * rp + 256)
+W_PARTS = {
+    "A0": [(0, 0, 0, 256, 0), (1, 256, 256, 256, 256)],
+    "A1": [(0, 256, 0, 512, 0)],
+    "A2": [(1, 256, 512, 512, 0)],
+    "B0": [(0, 512, 0, 512, 0)],
+    "B1": [(0, 768, 0, 512, 0)],
+    "B2": [(0, 768, 512, 512, 0)],
+    "B3": [(0, 512, 512, 256, 0), (1, 768, 768, 256, 256)],
+    "B4": [(1, 512, 512, 512, 0)],
+}
+W_MASKED = {"A0": (0, 512), "A1": (256, 512), "B2": (256, 512), "B3": (0, 512), "B4": (0, 256)}
+W_DEST = {
+    "A0": [(0, 64, 0, 0), (64, 128, 1, 0)],
+    "A1": [(0, 128, 0, 1)],
+    "A2": [(0, 128, 1, 1)],
+    "B0": [(0, 128, 2, 0)],
+    "B1": [(0, 128, 2, 1)],
+    "B2": [(0, 128, 3, 1)],
+    "B3": [(0, 64, 3, 0), (64, 128, 4, 1)],
+    "B4": [(0, 128, 4, 0)],
+}
 
 
 def tile_cp_sparse_degree_lu_pa_t_kernel(tc, z, U_lo, masks_lo, out):
@@ -67,8 +56,7 @@ def tile_cp_sparse_degree_lu_pa_t_kernel(tc, z, U_lo, masks_lo, out):
         zrun = ctx.enter_context(tc.tile_pool(name="zrun", bufs=4))
         outp = ctx.enter_context(tc.tile_pool(name="outp", bufs=OUT_BUFS))
         psum = ctx.enter_context(tc.psum_pool(name="psum", bufs=8))
-        if PIN:
-            ctx.enter_context(tc.manual_schedule())
+        ctx.enter_context(tc.manual_schedule())
 
         count = [0]
 
@@ -85,40 +73,36 @@ def tile_cp_sparse_degree_lu_pa_t_kernel(tc, z, U_lo, masks_lo, out):
         ident = const.tile([P, P], F32, name="ident")
         make_identity(nc, ident[:])
 
-        pairs_a = [(0, 0), (0, 1), (1, 1)]
-        pairs_b = [(0, 2), (0, 3), (1, 2), (1, 3)]
         raws = {}
         msks = {}
-        for key in pairs_a + pairs_b:
-            i, rp = key
-            s0, s1 = spec_range(i, rp)
-            m0, m1 = mask_range(i, rp)
-            raws[key] = const.tile([P, 2 * (s1 - s0)], BF16, name="raw%d%d" % key)
-            msks[key] = const.tile([P, 2 * (m1 - m0)], BF16, name="msk%d%d" % key)
-            l0, l1 = live_range(i, rp)
-            r3 = raws[key][:].rearrange("p (r c) -> p r c", r=2)
-            if l0 > s0:
-                nc.vector.memset(r3[:, :, 0 : l0 - s0], 0.0)
-            if l1 < s1:
-                nc.vector.memset(r3[:, :, l1 - s0 : s1 - s0], 0.0)
+        for key in W_PARTS:
+            raws[key] = const.tile([P, 1024], BF16, name="raw" + key)
+            if key in W_MASKED:
+                m0, m1 = W_MASKED[key]
+                msks[key] = const.tile([P, 2 * (m1 - m0)], BF16, name="msk" + key)
         wg = [const.tile([P, 2048], BF16, name="wg%d" % s, align_bytes=64) for s in range(5)]
         wc = [const.tile([P, 512], U32, name="wc%d" % s, align_bytes=64) for s in range(5)]
         ws = [const.tile([P, 512], U8, name="ws%d" % s, align_bytes=64) for s in range(5)]
+        for key, eng in (("A0", nc.vector), ("B3", nc.gpsimd)):
+            for p0, p1, s, half in W_DEST[key]:
+                eng.memset(wg[s][P - p1 : P - p0, 1024 * half : 1024 * half + 1024], 0.0)
+
+        def load_part(dst, dram, part):
+            i, rank, feat, n, col = part
+            nc.sync.dma_start(
+                out=dst[:].rearrange("p (r c) -> p r c", r=2)[:, :, col : col + n],
+                in_=dram[i, rank : rank + 256, feat : feat + n].rearrange("(r p) c -> p r c", p=P),
+            )
 
         def load_w(key):
-            i, rp = key
-            s0, s1 = spec_range(i, rp)
-            m0, m1 = mask_range(i, rp)
-            l0, l1 = live_range(i, rp)
-            rows = slice(256 * rp, 256 * rp + 256)
-            nc.sync.dma_start(
-                out=msks[key][:].rearrange("p (r c) -> p r c", r=2),
-                in_=masks_lo[i, rows, m0:m1].rearrange("(r p) c -> p r c", p=P),
-            )
-            nc.sync.dma_start(
-                out=raws[key][:].rearrange("p (r c) -> p r c", r=2)[:, :, l0 - s0 : l1 - s0],
-                in_=U_lo[i, rows, l0:l1].rearrange("(r p) c -> p r c", p=P),
-            )
+            for part in W_PARTS[key]:
+                if key in W_MASKED:
+                    i, rank, feat, n, col = part
+                    m0, m1 = W_MASKED[key]
+                    lo = max(m0, col)
+                    hi = min(m1, col + n)
+                    load_part(msks[key], masks_lo, (i, rank, feat + lo - col, hi - lo, lo - m0))
+                load_part(raws[key], U_lo, part)
 
         zraw = [zin.tile([P, GROUP * FEATS], BF16, name="zraw%d" % g, tag="zraw") for g in range(N_GROUPS)]
 
@@ -127,47 +111,55 @@ def tile_cp_sparse_degree_lu_pa_t_kernel(tc, z, U_lo, masks_lo, out):
             dst = zraw[grp][:].rearrange("p (j c) -> p j c", j=GROUP)
             nc.sync.dma_start(out=dst[:, j0:j1, :], in_=src[:, j0:j1, :])
 
-        for key in pairs_a:
-            load_w(key)
         load_z(0, 0, 2)
+        for key in ("A0", "A1", "A2"):
+            load_w(key)
         load_z(0, 2, 4)
-        for key in pairs_b:
+        for key in ("B0", "B1", "B2", "B3", "B4"):
             load_w(key)
         for grp in range(1, N_GROUPS):
             load_z(grp, 0, GROUP)
 
-        def mask_mult(i, rp):
-            s0, s1 = spec_range(i, rp)
-            m0, m1 = mask_range(i, rp)
-            part = raws[(i, rp)][:].rearrange("p (r c) -> p r c", r=2)[:, :, m0 - s0 : m1 - s0]
+        def w_mask(key):
+            m0, m1 = W_MASKED[key]
+            part = raws[key][:].rearrange("p (r c) -> p r c", r=2)[:, :, m0:m1]
             nc.vector.tensor_tensor(
-                out=part, in0=part, in1=msks[(i, rp)][:].rearrange("p (r c) -> p r c", r=2), op=ALU.mult
+                out=part, in0=part, in1=msks[key][:].rearrange("p (r c) -> p r c", r=2), op=ALU.mult
             )
+
+        wr = {}
+
+        def w_reorder(key):
+            t = const.tile([P, 1024], BF16, name="wr" + key)
+            nc.vector.tensor_copy(
+                out=t[:].bitcast(F32).rearrange("p (u w) -> p u w", u=2),
+                in_=raws[key][:].bitcast(F32).rearrange("p (w u) -> p u w", u=2),
+            )
+            wr[key] = t
 
         held = {}
 
-        def w_transposes(n):
-            i, g, rp, s, half = W_BANKS[n]
-            s0, s1 = spec_range(i, rp)
-            words = (s1 - s0) // 2
-            rawf = raws[(i, rp)][:].bitcast(F32)
+        def w_transposes(key):
             bk = bank()
             for u in range(2):
                 for r in range(2):
-                    w0 = r * words + (512 * g - s0) // 2 + u
+                    if key in wr:
+                        w0 = 256 * u + P * r
+                        words = wr[key][:].bitcast(F32)[:, w0 : w0 + P]
+                    else:
+                        w0 = 256 * r + u
+                        words = raws[key][:].bitcast(F32)[:, w0 : w0 + 2 * P - 1 : 2]
                     nc.tensor.transpose(
-                        out=bk[:, 256 * u + P * r : 256 * u + P * r + P],
-                        in_=rawf[:, w0 : w0 + 2 * P - 1 : 2],
-                        identity=ident[:],
+                        out=bk[:, 256 * u + P * r : 256 * u + P * r + P], in_=words, identity=ident[:]
                     )
-            held[("w", n)] = bk
+            held[key] = bk
 
-        def w_copy(n, eng):
-            i, g, rp, s, half = W_BANKS[n]
+        def w_copy(key, n, eng):
+            p0, p1, s, half = W_DEST[key][n]
             copy_out(
                 eng,
-                wg[s][:].bitcast(F32)[:, 512 * half : 512 * half + 512].rearrange("p (r u) -> p r u", u=2),
-                held[("w", n)][:].rearrange("p (u r) -> p r u", u=2),
+                wg[s][:].bitcast(F32)[p0:p1, 512 * half : 512 * half + 512].rearrange("p (r u) -> p r u", u=2),
+                held[key][p0:p1, :].rearrange("p (u r) -> p r u", u=2),
             )
 
         def w_quant(s):
@@ -322,61 +314,59 @@ def tile_cp_sparse_degree_lu_pa_t_kernel(tc, z, U_lo, masks_lo, out):
             if not is_fine(grp, h):
                 store_pair(grp, h)
 
-        mask_mult(0, 0)
-        w_transposes(0)
-        mask_mult(0, 1)
-        w_copy(0, "v")
-        mask_mult(1, 1)
-        w_transposes(1)
-        w_transposes(2)
-        w_transposes(3)
-        w_copy(1, "s")
-        w_copy(2, "s")
-        w_quant(0)
         z_transposes(0, 0)
         z_transposes(0, 1)
-        z_copy(0, 1, "v")
+        w_mask("A0")
+        w_transposes("A0")
         z_copy(0, 0, "s")
-        w_copy(3, "s")
+        z_copy(0, 1, "s")
+        w_mask("A1")
+        w_copy("A0", 0, "v")
+        w_transposes("A1")
+        w_transposes("A2")
+        z_quant(0, 0)
+        w_copy("A1", 0, "s")
+        w_copy("A2", 0, "s")
+        w_quant(0)
         z_transposes(0, 2)
         z_transposes(0, 3)
-        z_quant(0, 0)
+        w_copy("A0", 1, "v")
+        mx_y0a(0, 0)
         w_quant(1)
         z_copy(0, 2, "s")
         z_copy(0, 3, "s")
-        mask_mult(0, 2)
-        mask_mult(0, 3)
-        mx_a(0, 0)
-        out_y0a(0, 0)
+        mx_y1a(0, 0)
         z_quant(0, 1)
-        for n in range(4, 8):
-            w_transposes(n)
+        out_y0a(0, 0)
+        w_mask("B2")
+        for key in ("B0", "B1", "B2"):
+            w_transposes(key)
+        w_mask("B3")
+        w_mask("B4")
         out_y1a(0, 0)
-        mask_mult(1, 2)
-        mask_mult(1, 3)
-        w_copy(4, "s")
-        w_copy(5, "v")
+        w_copy("B0", 0, "s")
+        w_copy("B1", 0, "v")
         mx_a(0, 1)
-        w_copy(6, "s")
-        w_copy(7, "v")
-        w_transposes(8)
-        w_transposes(9)
+        w_copy("B2", 0, "v")
+        w_transposes("B3")
+        w_transposes("B4")
         w_quant(2)
         out_y0a(0, 1)
         out_y1a(0, 1)
-        w_copy(8, "s")
-        w_copy(9, "s")
+        w_copy("B3", 0, "s")
+        w_copy("B3", 1, "s")
         w_quant(3)
+        w_copy("B4", 0, "s")
         for j in range(GROUP):
             z_transposes(1, j)
         w_quant(4)
         for j in range(GROUP):
             z_copy(1, j, "svsv"[j])
+        z_reorder(2, 0)
+        z_reorder(2, 1)
         mx_b(0, 0)
         z_quant(1, 0)
         out_b(0, 0)
-        z_reorder(2, 0)
-        z_reorder(2, 1)
         mx_b(0, 1)
         z_quant(1, 1)
         out_b(0, 1)
@@ -392,7 +382,15 @@ def tile_cp_sparse_degree_lu_pa_t_kernel(tc, z, U_lo, masks_lo, out):
                 out_a(first, h)
                 if nxt + 1 < N_GROUPS:
                     z_reorder(nxt + 1, h)
-                mx_b(first, h)
-                if nxt < N_GROUPS:
-                    z_quant(nxt, h)
-                out_b(first, h)
+                if first == N_GROUPS - 1:
+                    for jj in range(2):
+                        mx_y0b(first, h, jj)
+                        mx_y1b(first, h, jj)
+                        out_y0b(first, h, jj)
+                        out_y1b(first, h, jj)
+                        store(first, h, jj, jj + 1, 512, RANKS)
+                else:
+                    mx_b(first, h)
+                    if nxt < N_GROUPS:
+                        z_quant(nxt, h)
+                    out_b(first, h)

@@ -23,17 +23,24 @@ BYTES = TOKENS * FEATS * 2 + TOKENS * RANKS * 4 + 2 * 1310720 * 2
 OUT_BUFS = 6
 FINE_PAIRS = 3
 
-W_PARTS = {
-    "A0": [(0, 0, 0, 256, 0), (1, 256, 256, 256, 256)],
-    "A1": [(0, 256, 0, 512, 0)],
-    "A2": [(1, 256, 512, 512, 0)],
-    "B0": [(0, 512, 0, 512, 0)],
-    "B1": [(0, 768, 0, 512, 0)],
-    "B2": [(0, 768, 512, 512, 0)],
-    "B3": [(0, 512, 512, 256, 0), (1, 768, 768, 256, 256)],
-    "B4": [(1, 512, 512, 512, 0)],
+W_TILES = {
+    "A": (1024, [(0, 0, 0, 256, 0), (1, 256, 256, 256, 256), (1, 256, 512, 512, 512)]),
+    "A1": (512, [(0, 256, 0, 512, 0)]),
+    "B": (1024, [(0, 512, 0, 768, 0), (1, 768, 768, 256, 768)]),
+    "C": (1024, [(0, 768, 0, 1024, 0)]),
+    "B4": (512, [(1, 512, 512, 512, 0)]),
 }
-W_MASKED = {"A0": (0, 512), "A1": (256, 512), "B2": (256, 512), "B3": (0, 512), "B4": (0, 256)}
+W_BANKS = {
+    "A0": ("A", 0),
+    "A1": ("A1", 0),
+    "A2": ("A", 512),
+    "B0": ("B", 0),
+    "B1": ("C", 0),
+    "B2": ("C", 512),
+    "B3": ("B", 512),
+    "B4": ("B4", 0),
+}
+W_MASKED = {"A0": (0, 512, 0), "A1": (256, 512, 0), "B2": (256, 512, 0), "B3": (0, 512, 0), "B4": (0, 256, 256)}
 W_DEST = {
     "A0": [(0, 64, 0, 0), (64, 128, 1, 0)],
     "A1": [(0, 128, 0, 1)],
@@ -73,13 +80,8 @@ def tile_cp_sparse_degree_lu_pa_t_kernel(tc, z, U_lo, masks_lo, out):
         ident = const.tile([P, P], F32, name="ident")
         make_identity(nc, ident[:])
 
-        raws = {}
-        msks = {}
-        for key in W_PARTS:
-            raws[key] = const.tile([P, 1024], BF16, name="raw" + key)
-            if key in W_MASKED:
-                m0, m1 = W_MASKED[key]
-                msks[key] = const.tile([P, 2 * (m1 - m0)], BF16, name="msk" + key)
+        raws = {name: const.tile([P, 2 * W_TILES[name][0]], BF16, name="raw" + name) for name in W_TILES}
+        msk = const.tile([P, 1024], BF16, name="msk")
         wg = [const.tile([P, 2048], BF16, name="wg%d" % s, align_bytes=64) for s in range(5)]
         wc = [const.tile([P, 512], U32, name="wc%d" % s, align_bytes=64) for s in range(5)]
         ws = [const.tile([P, 512], U8, name="ws%d" % s, align_bytes=64) for s in range(5)]
@@ -94,15 +96,8 @@ def tile_cp_sparse_degree_lu_pa_t_kernel(tc, z, U_lo, masks_lo, out):
                 in_=dram[i, rank : rank + 256, feat : feat + n].rearrange("(r p) c -> p r c", p=P),
             )
 
-        def load_w(key):
-            for part in W_PARTS[key]:
-                if key in W_MASKED:
-                    i, rank, feat, n, col = part
-                    m0, m1 = W_MASKED[key]
-                    lo = max(m0, col)
-                    hi = min(m1, col + n)
-                    load_part(msks[key], masks_lo, (i, rank, feat + lo - col, hi - lo, lo - m0))
-                load_part(raws[key], U_lo, part)
+        def load_w(name, k):
+            load_part(raws[name], U_lo, W_TILES[name][1][k])
 
         zraw = [zin.tile([P, GROUP * FEATS], BF16, name="zraw%d" % g, tag="zraw") for g in range(N_GROUPS)]
 
@@ -112,29 +107,39 @@ def tile_cp_sparse_degree_lu_pa_t_kernel(tc, z, U_lo, masks_lo, out):
             nc.sync.dma_start(out=dst[:, j0:j1, :], in_=src[:, j0:j1, :])
 
         load_z(0, 0, 2)
-        for key in ("A0", "A1", "A2"):
-            load_w(key)
+        load_part(msk, masks_lo, (0, 0, 0, 256, 0))
+        load_w("A", 0)
+        load_part(msk, masks_lo, (1, 256, 256, 256, 256))
+        load_w("A", 1)
+        load_w("A1", 0)
+        load_w("A", 2)
         load_z(0, 2, 4)
-        for key in ("B0", "B1", "B2", "B3", "B4"):
-            load_w(key)
+        load_w("B", 0)
+        load_w("C", 0)
+        load_w("B", 1)
+        load_w("B4", 0)
         for grp in range(1, N_GROUPS):
             load_z(grp, 0, GROUP)
 
         def w_mask(key):
-            m0, m1 = W_MASKED[key]
-            part = raws[key][:].rearrange("p (r c) -> p r c", r=2)[:, :, m0:m1]
+            name, col = W_BANKS[key]
+            m0, m1, mc = W_MASKED[key]
+            part = raws[name][:].rearrange("p (r c) -> p r c", r=2)[:, :, col + m0 : col + m1]
             nc.vector.tensor_tensor(
-                out=part, in0=part, in1=msks[key][:].rearrange("p (r c) -> p r c", r=2), op=ALU.mult
+                out=part,
+                in0=part,
+                in1=msk[:].rearrange("p (r c) -> p r c", r=2)[:, :, mc : mc + m1 - m0],
+                op=ALU.mult,
             )
 
         wr = {}
 
         def w_reorder(key):
+            name, col = W_BANKS[key]
             t = const.tile([P, 1024], BF16, name="wr" + key)
-            nc.vector.tensor_copy(
-                out=t[:].bitcast(F32).rearrange("p (u w) -> p u w", u=2),
-                in_=raws[key][:].bitcast(F32).rearrange("p (w u) -> p u w", u=2),
-            )
+            src = raws[name][:].bitcast(F32).rearrange("p (r w) -> p r w", r=2)[:, :, col // 2 : col // 2 + 256]
+            dst = t[:].bitcast(F32).rearrange("p (r u w) -> p r u w", r=2, u=2)
+            nc.vector.tensor_copy(out=dst, in_=src.rearrange("p r (w u) -> p r u w", u=2))
             wr[key] = t
 
         held = {}
@@ -144,11 +149,12 @@ def tile_cp_sparse_degree_lu_pa_t_kernel(tc, z, U_lo, masks_lo, out):
             for u in range(2):
                 for r in range(2):
                     if key in wr:
-                        w0 = 256 * u + P * r
+                        w0 = 256 * r + P * u
                         words = wr[key][:].bitcast(F32)[:, w0 : w0 + P]
                     else:
-                        w0 = 256 * r + u
-                        words = raws[key][:].bitcast(F32)[:, w0 : w0 + 2 * P - 1 : 2]
+                        name, col = W_BANKS[key]
+                        w0 = (W_TILES[name][0] * r + col) // 2 + u
+                        words = raws[name][:].bitcast(F32)[:, w0 : w0 + 2 * P - 1 : 2]
                     nc.tensor.transpose(
                         out=bk[:, 256 * u + P * r : 256 * u + P * r + P], in_=words, identity=ident[:]
                     )
@@ -316,25 +322,25 @@ def tile_cp_sparse_degree_lu_pa_t_kernel(tc, z, U_lo, masks_lo, out):
 
         z_transposes(0, 0)
         z_transposes(0, 1)
+        z_copy(0, 0, "s")
+        z_copy(0, 1, "v")
         w_mask("A0")
         w_transposes("A0")
-        z_copy(0, 0, "s")
-        z_copy(0, 1, "s")
         w_mask("A1")
-        w_copy("A0", 0, "v")
+        z_quant(0, 0)
+        w_copy("A0", 0, "s")
         w_transposes("A1")
         w_transposes("A2")
-        z_quant(0, 0)
-        w_copy("A1", 0, "s")
-        w_copy("A2", 0, "s")
+        w_copy("A1", 0, "v")
+        w_copy("A0", 1, "s")
         w_quant(0)
+        w_copy("A2", 0, "s")
         z_transposes(0, 2)
         z_transposes(0, 3)
-        w_copy("A0", 1, "v")
         mx_y0a(0, 0)
-        w_quant(1)
-        z_copy(0, 2, "s")
+        z_copy(0, 2, "v")
         z_copy(0, 3, "s")
+        w_quant(1)
         mx_y1a(0, 0)
         z_quant(0, 1)
         out_y0a(0, 0)
@@ -342,14 +348,17 @@ def tile_cp_sparse_degree_lu_pa_t_kernel(tc, z, U_lo, masks_lo, out):
         for key in ("B0", "B1", "B2"):
             w_transposes(key)
         w_mask("B3")
+        w_reorder("B3")
         w_mask("B4")
+        w_reorder("B4")
         out_y1a(0, 0)
         w_copy("B0", 0, "s")
-        w_copy("B1", 0, "v")
+        w_copy("B1", 0, "s")
         mx_a(0, 1)
         w_copy("B2", 0, "v")
         w_transposes("B3")
         w_transposes("B4")
+        z_reorder(1, 1)
         w_quant(2)
         out_y0a(0, 1)
         out_y1a(0, 1)

@@ -322,24 +322,24 @@ def tile_cp_sparse_degree_lu_pa_t_kernel(tc, z, U_lo, masks_lo, out):
 
         z_transposes(0, 0)
         z_transposes(0, 1)
-        z_copy(0, 0, "s")
-        z_copy(0, 1, "v")
         w_mask("A0")
         w_transposes("A0")
+        z_copy(0, 0, "s")
+        z_copy(0, 1, "s")
         w_mask("A1")
-        z_quant(0, 0)
-        w_copy("A0", 0, "s")
+        w_copy("A0", 0, "v")
         w_transposes("A1")
         w_transposes("A2")
-        w_copy("A1", 0, "v")
-        w_copy("A0", 1, "s")
-        w_quant(0)
+        z_quant(0, 0)
+        w_copy("A1", 0, "s")
         w_copy("A2", 0, "s")
+        w_quant(0)
         z_transposes(0, 2)
         z_transposes(0, 3)
         mx_y0a(0, 0)
-        z_copy(0, 2, "v")
+        z_copy(0, 2, "s")
         z_copy(0, 3, "s")
+        w_copy("A0", 1, "v")
         w_quant(1)
         mx_y1a(0, 0)
         z_quant(0, 1)
@@ -384,11 +384,14 @@ def tile_cp_sparse_degree_lu_pa_t_kernel(tc, z, U_lo, masks_lo, out):
             if nxt < N_GROUPS:
                 for j in range(GROUP):
                     z_transposes(nxt, j)
-                for j in range(GROUP):
-                    z_copy(nxt, j, "svsv"[j])
+                for j in range(3):
+                    z_copy(nxt, j, "ssvs"[j])
             for h in range(2):
                 mx_a(first, h)
                 out_a(first, h)
+                if h == 0 and nxt < N_GROUPS:
+                    for j in range(3, GROUP):
+                        z_copy(nxt, j, "ssvs"[j])
                 if nxt + 1 < N_GROUPS:
                     z_reorder(nxt + 1, h)
                 if first == N_GROUPS - 1:

@@ -82,6 +82,9 @@ def tile_cp_sparse_degree_lu_pa_t_kernel(tc, z, U_lo, masks_lo, out):
 
         raws = {name: const.tile([P, 2 * W_TILES[name][0]], BF16, name="raw" + name) for name in W_TILES}
         msk = const.tile([P, 1024], BF16, name="msk")
+        nc.vector.memset(msk[:, 128:256], 0.0)
+        nc.vector.memset(msk[:, 384:640], 1.0)
+        nc.vector.memset(msk[:, 768:896], 0.0)
         wg = [const.tile([P, 2048], BF16, name="wg%d" % s, align_bytes=64) for s in range(5)]
         wc = [const.tile([P, 512], U32, name="wc%d" % s, align_bytes=64) for s in range(5)]
         ws = [const.tile([P, 512], U8, name="ws%d" % s, align_bytes=64) for s in range(5)]
@@ -107,9 +110,9 @@ def tile_cp_sparse_degree_lu_pa_t_kernel(tc, z, U_lo, masks_lo, out):
             nc.sync.dma_start(out=dst[:, j0:j1, :], in_=src[:, j0:j1, :])
 
         load_z(0, 0, 2)
-        load_part(msk, masks_lo, (0, 0, 0, 256, 0))
+        nc.sync.dma_start(out=msk[:, 0:128], in_=masks_lo[0, 0:128, 0:128])
         load_w("A", 0)
-        load_part(msk, masks_lo, (1, 256, 256, 256, 256))
+        nc.sync.dma_start(out=msk[:, 256:384], in_=masks_lo[1, 256:384, 256:384])
         load_w("A", 1)
         load_w("A1", 0)
         load_w("A", 2)
@@ -322,6 +325,8 @@ def tile_cp_sparse_degree_lu_pa_t_kernel(tc, z, U_lo, masks_lo, out):
 
         z_transposes(0, 0)
         z_transposes(0, 1)
+        nc.vector.tensor_copy(out=msk[:, 640:768], in_=msk[:, 0:128])
+        nc.vector.tensor_copy(out=msk[:, 896:1024], in_=msk[:, 256:384])
         w_mask("A0")
         w_transposes("A0")
         z_copy(0, 0, "s")
@@ -337,10 +342,10 @@ def tile_cp_sparse_degree_lu_pa_t_kernel(tc, z, U_lo, masks_lo, out):
         z_transposes(0, 2)
         z_transposes(0, 3)
         mx_y0a(0, 0)
-        z_copy(0, 2, "s")
+        w_copy("A0", 1, "s")
         z_copy(0, 3, "s")
-        w_copy("A0", 1, "v")
         w_quant(1)
+        z_copy(0, 2, "v")
         mx_y1a(0, 0)
         z_quant(0, 1)
         out_y0a(0, 0)
@@ -355,7 +360,7 @@ def tile_cp_sparse_degree_lu_pa_t_kernel(tc, z, U_lo, masks_lo, out):
         w_copy("B0", 0, "s")
         w_copy("B1", 0, "s")
         mx_a(0, 1)
-        w_copy("B2", 0, "v")
+        w_copy("B2", 0, "s")
         w_transposes("B3")
         w_transposes("B4")
         z_reorder(1, 1)
@@ -370,7 +375,7 @@ def tile_cp_sparse_degree_lu_pa_t_kernel(tc, z, U_lo, masks_lo, out):
             z_transposes(1, j)
         w_quant(4)
         for j in range(GROUP):
-            z_copy(1, j, "svsv"[j])
+            z_copy(1, j, "ssvs"[j])
         z_reorder(2, 0)
         z_reorder(2, 1)
         mx_b(0, 0)

@@ -86,8 +86,8 @@ def tile_cp_sparse_degree_lu_pa_t_kernel(tc, z, U_lo, masks_lo, out):
         nc.vector.memset(msk[:, 384:640], 1.0)
         nc.vector.memset(msk[:, 768:896], 0.0)
         wg = [const.tile([P, 2048], BF16, name="wg%d" % s, align_bytes=64) for s in range(5)]
-        wc = [const.tile([P, 512], U32, name="wc%d" % s, align_bytes=64) for s in range(5)]
-        ws = [const.tile([P, 512], U8, name="ws%d" % s, align_bytes=64) for s in range(5)]
+        wc = [const.tile([P, 512], U32, name="wc%d" % s, align_bytes=256) for s in range(5)]
+        ws = [const.tile([P, 512], U8, name="ws%d" % s, align_bytes=256) for s in range(5)]
         for key, eng in (("A0", nc.vector), ("B3", nc.gpsimd)):
             for p0, p1, s, half in W_DEST[key]:
                 eng.memset(wg[s][P - p1 : P - p0, 1024 * half : 1024 * half + 1024], 0.0)
@@ -192,8 +192,8 @@ def tile_cp_sparse_degree_lu_pa_t_kernel(tc, z, U_lo, masks_lo, out):
         def z_transposes(grp, j):
             if j == 0:
                 zg[grp] = zwork.tile([P, GROUP * FEATS], BF16, name="zg%d" % grp, tag="zg", align_bytes=64)
-                zc[grp] = zwork.tile([P, GROUP * 256], U32, name="zc%d" % grp, tag="zc", align_bytes=64)
-                zs[grp] = zwork.tile([P, GROUP * 256], U8, name="zs%d" % grp, tag="zs", align_bytes=64)
+                zc[grp] = zwork.tile([P, GROUP * 256], U32, name="zc%d" % grp, tag="zc", align_bytes=256)
+                zs[grp] = zwork.tile([P, GROUP * 256], U8, name="zs%d" % grp, tag="zs", align_bytes=256)
             zrf = zraw[grp][:].bitcast(F32)
             bk = bank()
             for c in range(4):
@@ -347,9 +347,9 @@ def tile_cp_sparse_degree_lu_pa_t_kernel(tc, z, U_lo, masks_lo, out):
         w_quant(1)
         z_copy(0, 2, "v")
         mx_y1a(0, 0)
+        w_mask("B2")
         z_quant(0, 1)
         out_y0a(0, 0)
-        w_mask("B2")
         for key in ("B0", "B1", "B2"):
             w_transposes(key)
         w_mask("B3")

@@ -386,7 +386,8 @@ def tile_cp_sparse_degree_lu_pa_t_kernel(tc, z, U_lo, masks_lo, out):
         out_b(0, 1)
         for first in range(1, N_GROUPS):
             nxt = first + 1
-            if nxt < N_GROUPS:
+            split = first == N_GROUPS - 2
+            if nxt < N_GROUPS and not split:
                 for j in range(GROUP):
                     z_transposes(nxt, j)
                 for j in range(3):
@@ -394,9 +395,8 @@ def tile_cp_sparse_degree_lu_pa_t_kernel(tc, z, U_lo, masks_lo, out):
             for h in range(2):
                 mx_a(first, h)
                 out_a(first, h)
-                if h == 0 and nxt < N_GROUPS:
-                    for j in range(3, GROUP):
-                        z_copy(nxt, j, "ssvs"[j])
+                if h == 0 and nxt < N_GROUPS and not split:
+                    z_copy(nxt, 3, "s")
                 if nxt + 1 < N_GROUPS:
                     z_reorder(nxt + 1, h)
                 if first == N_GROUPS - 1:
@@ -405,9 +405,19 @@ def tile_cp_sparse_degree_lu_pa_t_kernel(tc, z, U_lo, masks_lo, out):
                         mx_y1b(first, h, jj)
                         out_y0b(first, h, jj)
                         out_y1b(first, h, jj)
-                        store(first, h, jj, jj + 1, 512, RANKS)
+                        if is_fine(first, h):
+                            store(first, h, jj, jj + 1, 512, RANKS)
+                    if not is_fine(first, h):
+                        store_pair(first, h)
                 else:
                     mx_b(first, h)
-                    if nxt < N_GROUPS:
+                    if nxt < N_GROUPS and not split:
                         z_quant(nxt, h)
+                    if split:
+                        for j in (2 * h, 2 * h + 1):
+                            z_transposes(nxt, j)
                     out_b(first, h)
+                    if split:
+                        for j in (2 * h, 2 * h + 1):
+                            z_copy(nxt, j, "sv"[j % 2])
+                        z_quant(nxt, h)

@@ -390,13 +390,11 @@ def tile_cp_sparse_degree_lu_pa_t_kernel(tc, z, U_lo, masks_lo, out):
             if nxt < N_GROUPS and not split:
                 for j in range(GROUP):
                     z_transposes(nxt, j)
-                for j in range(3):
-                    z_copy(nxt, j, "ssvs"[j])
+                for j in range(GROUP):
+                    z_copy(nxt, j, "svsv"[j])
             for h in range(2):
                 mx_a(first, h)
                 out_a(first, h)
-                if h == 0 and nxt < N_GROUPS and not split:
-                    z_copy(nxt, 3, "s")
                 if nxt + 1 < N_GROUPS:
                     z_reorder(nxt + 1, h)
                 if first == N_GROUPS - 1:

from contextlib import ExitStack

import concourse.mybir as mybir
from concourse.masks import make_identity

F32 = mybir.dt.float32
BF16 = mybir.dt.bfloat16
U32 = mybir.dt.uint32
U8 = mybir.dt.uint8
FP8X4 = mybir.dt.float8_e4m3fn_x4
ALU = mybir.AluOpType

P = 128
TOKENS = 4096
FEATS = 1024
RANKS = 1024
GROUP = 4
N_GROUPS = TOKENS // (P * GROUP)

FLOPS = 2 * TOKENS * 1310720
BYTES = TOKENS * FEATS * 2 + TOKENS * RANKS * 4 + 2 * 1310720 * 2

OUT_BUFS = 6
FINE_PAIRS = 3

W_TILES = {
    "A": (1024, [(0, 0, 0, 256, 0), (1, 256, 256, 256, 256), (1, 256, 512, 512, 512)]),
    "A1": (512, [(0, 256, 0, 512, 0)]),
    "B": (1024, [(0, 512, 0, 768, 0), (1, 768, 768, 256, 768)]),
    "C": (1024, [(0, 768, 0, 1024, 0)]),
    "B4": (512, [(1, 512, 512, 512, 0)]),
}
W_BANKS = {
    "A0": ("A", 0),
    "A1": ("A1", 0),
    "A2": ("A", 512),
    "B0": ("B", 0),
    "B1": ("C", 0),
    "B2": ("C", 512),
    "B3": ("B", 512),
    "B4": ("B4", 0),
}
W_MASKED = {"A0": (0, 512, 0), "A1": (256, 512, 0), "B2": (256, 512, 0), "B3": (0, 512, 0), "B4": (0, 256, 256)}
W_DEST = {
    "A0": [(0, 64, 0, 0), (64, 128, 1, 0)],
    "A1": [(0, 128, 0, 1)],
    "A2": [(0, 128, 1, 1)],
    "B0": [(0, 128, 2, 0)],
    "B1": [(0, 128, 2, 1)],
    "B2": [(0, 128, 3, 1)],
    "B3": [(0, 64, 3, 0), (64, 128, 4, 1)],
    "B4": [(0, 128, 4, 0)],
}


def tile_cp_sparse_degree_lu_pa_t_kernel(tc, z, U_lo, masks_lo, out):
    nc = tc.nc
    zf = z.flatten_outer_dims()
    with ExitStack() as ctx:
        const = ctx.enter_context(tc.tile_pool(name="const", bufs=1))
        zin = ctx.enter_context(tc.tile_pool(name="zin", bufs=N_GROUPS))
        zwork = ctx.enter_context(tc.tile_pool(name="zwork", bufs=3))
        zrun = ctx.enter_context(tc.tile_pool(name="zrun", bufs=4))
        outp = ctx.enter_context(tc.tile_pool(name="outp", bufs=OUT_BUFS))
        psum = ctx.enter_context(tc.psum_pool(name="psum", bufs=8))
        ctx.enter_context(tc.manual_schedule())

        count = [0]

        def bank():
            count[0] += 1
            return psum.tile([P, 512], F32, name="bank%d" % count[0], tag="bank")

        def copy_out(eng, dst, src):
            if eng == "s":
                nc.scalar.copy(out=dst, in_=src)
            else:
                nc.vector.tensor_copy(out=dst, in_=src)

        ident = const.tile([P, P], F32, name="ident")
        make_identity(nc, ident[:])

        raws = {name: const.tile([P, 2 * W_TILES[name][0]], BF16, name="raw" + name) for name in W_TILES}
        msk = const.tile([P, 1024], BF16, name="msk")
        nc.vector.memset(msk[:, 128:256], 0.0)
        nc.vector.memset(msk[:, 384:640], 1.0)
        nc.vector.memset(msk[:, 768:896], 0.0)
        wg = [const.tile([P, 2048], BF16, name="wg%d" % s, align_bytes=64) for s in range(5)]
        wc = [const.tile([P, 512], U32, name="wc%d" % s, align_bytes=256) for s in range(5)]
        ws = [const.tile([P, 512], U8, name="ws%d" % s, align_bytes=256) for s in range(5)]
        for key, eng in (("A0", nc.vector), ("B3", nc.gpsimd)):
            for p0, p1, s, half in W_DEST[key]:
                eng.memset(wg[s][P - p1 : P - p0, 1024 * half : 1024 * half + 1024], 0.0)

        def load_part(dst, dram, part):
            i, rank, feat, n, col = part
            nc.sync.dma_start(
                out=dst[:].rearrange("p (r c) -> p r c", r=2)[:, :, col : col + n],
                in_=dram[i, rank : rank + 256, feat : feat + n].rearrange("(r p) c -> p r c", p=P),
            )

        def load_w(name, k):
            load_part(raws[name], U_lo, W_TILES[name][1][k])

        zraw = [zin.tile([P, GROUP * FEATS], BF16, name="zraw%d" % g, tag="zraw") for g in range(N_GROUPS)]

        def load_z(grp, j0, j1):
            src = zf[512 * grp : 512 * grp + 512, :].rearrange("(p j) c -> p j c", j=GROUP)
            dst = zraw[grp][:].rearrange("p (j c) -> p j c", j=GROUP)
            nc.sync.dma_start(out=dst[:, j0:j1, :], in_=src[:, j0:j1, :])

        load_z(0, 0, 2)
        nc.sync.dma_start(out=msk[:, 0:128], in_=masks_lo[0, 0:128, 0:128])
        load_w("A", 0)
        nc.sync.dma_start(out=msk[:, 256:384], in_=masks_lo[1, 256:384, 256:384])
        load_w("A", 1)
        load_w("A1", 0)
        load_w("A", 2)
        load_z(0, 2, 4)
        load_w("B", 0)
        load_w("C", 0)
        load_w("B", 1)
        load_w("B4", 0)
        for grp in range(1, N_GROUPS):
            load_z(grp, 0, GROUP)

        def w_mask(key):
            name, col = W_BANKS[key]
            m0, m1, mc = W_MASKED[key]
            part = raws[name][:].rearrange("p (r c) -> p r c", r=2)[:, :, col + m0 : col + m1]
            nc.vector.tensor_tensor(
                out=part,
                in0=part,
                in1=msk[:].rearrange("p (r c) -> p r c", r=2)[:, :, mc : mc + m1 - m0],
                op=ALU.mult,
            )

        wr = {}

        def w_reorder(key):
            name, col = W_BANKS[key]
            t = const.tile([P, 1024], BF16, name="wr" + key)
            src = raws[name][:].bitcast(F32).rearrange("p (r w) -> p r w", r=2)[:, :, col // 2 : col // 2 + 256]
            dst = t[:].bitcast(F32).rearrange("p (r u w) -> p r u w", r=2, u=2)
            nc.vector.tensor_copy(out=dst, in_=src.rearrange("p r (w u) -> p r u w", u=2))
            wr[key] = t

        held = {}

        def w_transposes(key):
            bk = bank()
            for u in range(2):
                for r in range(2):
                    if key in wr:
                        w0 = 256 * r + P * u
                        words = wr[key][:].bitcast(F32)[:, w0 : w0 + P]
                    else:
                        name, col = W_BANKS[key]
                        w0 = (W_TILES[name][0] * r + col) // 2 + u
                        words = raws[name][:].bitcast(F32)[:, w0 : w0 + 2 * P - 1 : 2]
                    nc.tensor.transpose(
                        out=bk[:, 256 * u + P * r : 256 * u + P * r + P], in_=words, identity=ident[:]
                    )
            held[key] = bk

        def w_copy(key, n, eng):
            p0, p1, s, half = W_DEST[key][n]
            copy_out(
                eng,
                wg[s][:].bitcast(F32)[p0:p1, 512 * half : 512 * half + 512].rearrange("p (r u) -> p r u", u=2),
                held[key][p0:p1, :].rearrange("p (u r) -> p r u", u=2),
            )

        def w_quant(s):
            nc.vector.quantize_mx(out=wc[s][:].bitcast(FP8X4), scales=ws[s][:], in_=wg[s][:])

        zr = {}
        zg = {}
        zc = {}
        zs = {}

        def z_reorder(grp, h):
            t = zrun.tile([P, 2 * FEATS], BF16, name="zr%d%d" % (grp, h), tag="zr")
            nc.vector.tensor_copy(
                out=t[:].bitcast(F32).rearrange("p (g u q) -> p g u q", g=4, u=2),
                in_=zraw[grp][:, 2 * FEATS * h : 2 * FEATS * (h + 1)]
                .bitcast(F32)
                .rearrange("p (g q u) -> p g u q", g=4, u=2),
            )
            zr[(grp, h)] = t

        def z_transposes(grp, j):
            if j == 0:
                zg[grp] = zwork.tile([P, GROUP * FEATS], BF16, name="zg%d" % grp, tag="zg", align_bytes=64)
                zc[grp] = zwork.tile([P, GROUP * 256], U32, name="zc%d" % grp, tag="zc", align_bytes=256)
                zs[grp] = zwork.tile([P, GROUP * 256], U8, name="zs%d" % grp, tag="zs", align_bytes=256)
            zrf = zraw[grp][:].bitcast(F32)
            bk = bank()
            for c in range(4):
                if (grp, j // 2) in zr:
                    w0 = 512 * (j % 2) + P * c
                    words = zr[(grp, j // 2)][:].bitcast(F32)[:, w0 : w0 + P]
                else:
                    w0 = 512 * j + 256 * (c // 2) + c % 2
                    words = zrf[:, w0 : w0 + 2 * P - 1 : 2]
                nc.tensor.transpose(out=bk[:, P * c : P * c + P], in_=words, identity=ident[:])
            held[("z", grp, j)] = bk

        def z_copy(grp, j, eng):
            copy_out(
                eng,
                zg[grp][:].bitcast(F32)[:, 512 * j : 512 * j + 512].rearrange("p (g t u) -> p g t u", g=2, u=2),
                held[("z", grp, j)][:].rearrange("p (g u t) -> p g t u", g=2, u=2),
            )

        def z_quant(grp, h):
            nc.vector.quantize_mx(
                out=zc[grp][:, 512 * h : 512 * h + 512].bitcast(FP8X4),
                scales=zs[grp][:, 512 * h : 512 * h + 512],
                in_=zg[grp][:, 2048 * h : 2048 * h + 2048],
            )

        def mm(dst, grp, j, g, s, c0, c1, start, stop):
            a = 256 * j + P * g
            nc.tensor.matmul_mx(
                out=dst,
                lhsT=zc[grp][:, a : a + P].bitcast(FP8X4),
                lhsT_scale=zs[grp][:, a : a + P],
                rhs=wc[s][:, c0:c1].bitcast(FP8X4),
                rhs_scale=ws[s][:, c0:c1],
                start=start,
                stop=stop,
            )

        osb = {}

        def mx_y0a(grp, h):
            for jj in range(2):
                bk = bank()
                mm(bk[:], grp, 2 * h + jj, 0, 0, 0, 512, True, True)
                held[("y0a", grp, h, jj)] = bk

        def mx_y1a(grp, h):
            bk = bank()
            for jj in range(2):
                mm(bk[:, 256 * jj : 256 * jj + 256], grp, 2 * h + jj, 0, 1, 0, 256, True, False)
                mm(bk[:, 256 * jj : 256 * jj + 256], grp, 2 * h + jj, 1, 1, 256, 512, False, True)
            held[("y1a", grp, h)] = bk

        def mx_y0b(grp, h, jj):
            bk = bank()
            mm(bk[:], grp, 2 * h + jj, 0, 2, 0, 512, True, False)
            mm(bk[:], grp, 2 * h + jj, 1, 3, 0, 512, False, True)
            held[("y0b", grp, h, jj)] = bk

        def mx_y1b(grp, h, jj):
            bk = bank()
            mm(bk[:], grp, 2 * h + jj, 1, 4, 0, 512, True, True)
            held[("y1b", grp, h, jj)] = bk

        def out_y0a(grp, h):
            o = outp.tile([P, 2 * RANKS], F32, name="o%d%d" % (grp, h), tag="o")
            osb[(grp, h)] = o
            for jj in range(2):
                nc.scalar.copy(out=o[:, RANKS * jj : RANKS * jj + 512], in_=held[("y0a", grp, h, jj)][:])

        def out_y1a(grp, h):
            o3 = osb[(grp, h)][:].rearrange("p (j r) -> p j r", j=2)[:, :, 256:512]
            nc.vector.scalar_tensor_tensor(
                out=o3,
                in0=held[("y1a", grp, h)][:].rearrange("p (j r) -> p j r", j=2),
                scalar=1.0,
                in1=o3,
                op0=ALU.add,
                op1=ALU.mult,
            )

        def out_y0b(grp, h, jj):
            nc.scalar.copy(
                out=osb[(grp, h)][:, RANKS * jj + 512 : RANKS * jj + 1024], in_=held[("y0b", grp, h, jj)][:]
            )

        def out_y1b(grp, h, jj):
            part = osb[(grp, h)][:, RANKS * jj + 512 : RANKS * jj + 1024]
            nc.vector.scalar_tensor_tensor(
                out=part, in0=held[("y1b", grp, h, jj)][:], scalar=1.0, in1=part, op0=ALU.add, op1=ALU.mult
            )

        def store(grp, h, j0, j1, r0, r1):
            dst = out[512 * grp : 512 * grp + 512, :].rearrange("(p j) r -> p j r", j=GROUP)
            src = osb[(grp, h)][:].rearrange("p (j r) -> p j r", j=2)
            nc.sync.dma_start(out=dst[:, 2 * h + j0 : 2 * h + j1, r0:r1], in_=src[:, j0:j1, r0:r1])

        def store_pair(grp, h):
            store(grp, h, 0, 2, 0, RANKS)

        def is_fine(grp, h):
            return 2 * (N_GROUPS - 1 - grp) + (1 - h) < FINE_PAIRS

        def mx_a(grp, h):
            mx_y0a(grp, h)
            mx_y1a(grp, h)

        def out_a(grp, h):
            out_y0a(grp, h)
            out_y1a(grp, h)
            if is_fine(grp, h):
                store(grp, h, 0, 2, 0, 512)

        def mx_b(grp, h):
            for jj in range(2):
                mx_y0b(grp, h, jj)
            for jj in range(2):
                mx_y1b(grp, h, jj)

        def out_b(grp, h):
            for jj in range(2):
                out_y0b(grp, h, jj)
            for jj in range(2):
                out_y1b(grp, h, jj)
                if is_fine(grp, h):
                    store(grp, h, jj, jj + 1, 512, RANKS)
            if not is_fine(grp, h):
                store_pair(grp, h)

        z_transposes(0, 0)
        z_transposes(0, 1)
        nc.vector.tensor_copy(out=msk[:, 640:768], in_=msk[:, 0:128])
        nc.vector.tensor_copy(out=msk[:, 896:1024], in_=msk[:, 256:384])
        w_mask("A0")
        w_transposes("A0")
        z_copy(0, 0, "s")
        z_copy(0, 1, "s")
        w_mask("A1")
        w_copy("A0", 0, "v")
        w_transposes("A1")
        w_transposes("A2")
        z_quant(0, 0)
        w_copy("A1", 0, "s")
        w_copy("A2", 0, "s")
        w_quant(0)
        z_transposes(0, 2)
        z_transposes(0, 3)
        mx_y0a(0, 0)
        w_copy("A0", 1, "s")
        z_copy(0, 3, "s")
        w_quant(1)
        z_copy(0, 2, "v")
        mx_y1a(0, 0)
        w_mask("B2")
        z_quant(0, 1)
        out_y0a(0, 0)
        for key in ("B0", "B1", "B2"):
            w_transposes(key)
        w_mask("B3")
        w_reorder("B3")
        w_mask("B4")
        w_reorder("B4")
        out_y1a(0, 0)
        w_copy("B0", 0, "s")
        w_copy("B1", 0, "s")
        mx_a(0, 1)
        w_copy("B2", 0, "s")
        w_transposes("B3")
        w_transposes("B4")
        z_reorder(1, 1)
        w_quant(2)
        out_y0a(0, 1)
        out_y1a(0, 1)
        w_copy("B3", 0, "s")
        w_copy("B3", 1, "s")
        w_quant(3)
        w_copy("B4", 0, "s")
        for j in range(GROUP):
            z_transposes(1, j)
        w_quant(4)
        for j in range(GROUP):
            z_copy(1, j, "ssvs"[j])
        z_reorder(2, 0)
        z_reorder(2, 1)
        mx_b(0, 0)
        z_quant(1, 0)
        out_b(0, 0)
        mx_b(0, 1)
        z_quant(1, 1)
        out_b(0, 1)
        for first in range(1, N_GROUPS):
            nxt = first + 1
            split = first == N_GROUPS - 2
            if nxt < N_GROUPS and not split:
                for j in range(GROUP):
                    z_transposes(nxt, j)
                for j in range(GROUP):
                    z_copy(nxt, j, "svsv"[j])
            for h in range(2):
                mx_a(first, h)
                out_a(first, h)
                if nxt + 1 < N_GROUPS:
                    z_reorder(nxt + 1, h)
                if first == N_GROUPS - 1:
                    for jj in range(2):
                        mx_y0b(first, h, jj)
                        mx_y1b(first, h, jj)
                        out_y0b(first, h, jj)
                        out_y1b(first, h, jj)
                        if is_fine(first, h):
                            store(first, h, jj, jj + 1, 512, RANKS)
                    if not is_fine(first, h):
                        store_pair(first, h)
                else:
                    mx_b(first, h)
                    if nxt < N_GROUPS and not split:
                        z_quant(nxt, h)
                    if split:
                        for j in (2 * h, 2 * h + 1):
                            z_transposes(nxt, j)
                    out_b(first, h)
                    if split:
                        for j in (2 * h, 2 * h + 1):
                            z_copy(nxt, j, "sv"[j % 2])
                        z_quant(nxt, h)
